import numpy as np
import ml_dtypes


def mxq(x, axis, fmt="e4m3"):
    dtype, down = {"e4m3": (ml_dtypes.float8_e4m3fn, 7), "e5m2": (ml_dtypes.float8_e5m2, 14)}[fmt]
    v = np.moveaxis(np.asarray(x, np.float32).astype(ml_dtypes.bfloat16).astype(np.float64), axis, -1)
    blocks = v.reshape(v.shape[:-1] + (-1, 32))
    amax = np.abs(blocks).max(-1, keepdims=True)
    byte = np.maximum(np.where(amax > 0, np.frexp(amax)[1] - 1 + 127, 0) - down, 1)
    scale = np.exp2(byte - 127.0)
    codes = (blocks / scale).astype(np.float32).astype(dtype).astype(np.float64)
    return np.moveaxis((codes * scale).reshape(v.shape), -1, axis)


WIDE = False


def mx_kscale(k):
    if not WIDE:
        return np.ones(k)
    levels = np.array([10, -10, 5, -5, 0])
    a = np.random.permutation(np.resize(levels, k // 512 * 4)).reshape(k // 512, 4)
    idx = np.arange(k)
    return np.exp2(a[idx // 512, idx % 128 // 32])


BF16 = ml_dtypes.bfloat16


def bf(x):
    return np.asarray(x, np.float32).astype(BF16)


def f64(x):
    return np.asarray(x).astype(np.float64)


N, D_IN, D_HID, D_OUT = 4096, 256, 128, 128


def hamilton_Wq(Wr, Wi, Wj, Wk, xr, xi, xj, xk):
    x_cat = np.concatenate([xr, xi, xj, xk], axis=-1)
    n_in = Wr.shape[1]
    Wq = mxq(np.concatenate([Wr, Wi, Wj, Wk], axis=1), 1, "e4m3")
    Wr, Wi, Wj, Wk = Wq[:, :n_in], Wq[:, n_in:2 * n_in], Wq[:, 2 * n_in:3 * n_in], Wq[:, 3 * n_in:]
    W_block = np.concatenate([
        np.concatenate([Wr, Wi, Wj, Wk], axis=0),
        np.concatenate([-Wi, Wr, -Wk, Wj], axis=0),
        np.concatenate([-Wj, Wk, Wr, -Wi], axis=0),
        np.concatenate([-Wk, -Wj, Wi, Wr], axis=0),
    ], axis=1)
    h = mxq(x_cat, 1, "e4m3") @ W_block.T
    out = Wr.shape[0]
    return h[:, :out], h[:, out:2 * out], h[:, 2 * out:3 * out], h[:, 3 * out:]


def setup_inputs():
    s = mx_kscale(4 * D_IN)[:D_IN]
    t = mx_kscale(4 * D_HID)[:D_HID]
    inp = {}
    for c in "rijk":
        inp["q_" + c] = bf(np.random.standard_normal((N, D_IN)) * s)
    for c in "rijk":
        inp["W1_" + c] = bf(np.random.standard_normal((D_HID, D_IN)) * 0.5 / np.sqrt(D_IN) / s[None, :] * t[:, None])
    for c in "rijk":
        inp["b1_" + c] = bf(((0.0 if c == "r" else 0.2) + 0.1 * np.random.standard_normal(D_HID)) * t)
    for c in "rijk":
        inp["W2_" + c] = bf(np.random.standard_normal((D_OUT, D_HID)) * 0.7 / np.sqrt(D_HID) / t[None, :])
    for c in "rijk":
        inp["b2_" + c] = bf((0.0 if c == "r" else 0.2) + 0.1 * np.random.standard_normal(D_OUT))
    return inp


def reference(q_r, q_i, q_j, q_k,
              W1_r, W1_i, W1_j, W1_k, b1_r, b1_i, b1_j, b1_k,
              W2_r, W2_i, W2_j, W2_k, b2_r, b2_i, b2_j, b2_k):
    hr, hi, hj, hk = hamilton_Wq(f64(W1_r), f64(W1_i), f64(W1_j), f64(W1_k), f64(q_r), f64(q_i), f64(q_j), f64(q_k))
    hr = np.maximum(hr + f64(b1_r), 0.0)
    hi = np.maximum(hi + f64(b1_i), 0.0)
    hj = np.maximum(hj + f64(b1_j), 0.0)
    hk = np.maximum(hk + f64(b1_k), 0.0)
    or_, oi, oj, ok = hamilton_Wq(f64(W2_r), f64(W2_i), f64(W2_j), f64(W2_k), hr, hi, hj, hk)
    return (or_ + f64(b2_r), oi + f64(b2_i), oj + f64(b2_j), ok + f64(b2_k))

@@ -1,0 +1,217 @@
+from contextlib import ExitStack
+
+import concourse.mybir as mybir
+from concourse.masks import make_identity
+
+F32 = mybir.dt.float32
+BF16 = mybir.dt.bfloat16
+U32 = mybir.dt.uint32
+U8 = mybir.dt.uint8
+FP8X4 = mybir.dt.float8_e4m3fn_x4
+RELU = mybir.ActivationFunctionType.Relu
+ADD = mybir.AluOpType.add
+
+P = 128
+PACK = 4
+COMPS = 4
+ROWS = 4096
+D_IN = 256
+D_HID = 128
+D_OUT = 128
+IN_WORDS = D_IN // 2
+L1_PASSES = COMPS * D_IN // (P * PACK)
+SUB_ROWS = 4
+CHUNK = P * SUB_ROWS
+N_CHUNKS = ROWS // CHUNK
+QUADRANT = P // COMPS
+
+HAMILTON_SIGN = (
+    (1.0, -1.0, -1.0, -1.0),
+    (1.0, 1.0, 1.0, -1.0),
+    (1.0, -1.0, 1.0, 1.0),
+    (1.0, 1.0, -1.0, 1.0),
+)
+
+FLOPS = 2 * ROWS * (COMPS * D_IN) * (COMPS * D_HID) + 2 * ROWS * (COMPS * D_HID) * (COMPS * D_OUT)
+
+
+def pair_words(grouped_bf16):
+    return grouped_bf16.bitcast(F32).rearrange("p (a r u) -> p a r u", a=2, u=2)
+
+
+def tile_qmlp_t_kernel(
+    tc,
+    q_r, q_i, q_j, q_k,
+    W1_r, W1_i, W1_j, W1_k,
+    b1_r, b1_i, b1_j, b1_k,
+    W2_r, W2_i, W2_j, W2_k,
+    b2_r, b2_i, b2_j, b2_k,
+    out_0, out_1, out_2, out_3,
+):
+    nc = tc.nc
+    q = (q_r, q_i, q_j, q_k)
+    w1 = (W1_r, W1_i, W1_j, W1_k)
+    b1 = (b1_r, b1_i, b1_j, b1_k)
+    w2 = (W2_r, W2_i, W2_j, W2_k)
+    b2 = (b2_r, b2_i, b2_j, b2_k)
+    outs = (out_0, out_1, out_2, out_3)
+
+    with ExitStack() as stack:
+        const = stack.enter_context(tc.tile_pool(name="const", bufs=1))
+        q_pool = stack.enter_context(tc.tile_pool(name="q_rows", bufs=N_CHUNKS))
+        work = stack.enter_context(tc.tile_pool(name="work", bufs=2))
+        out_pool = stack.enter_context(tc.tile_pool(name="out_rows", bufs=3))
+        psum_t = stack.enter_context(tc.psum_pool(name="psum_t", bufs=3))
+        psum_h = stack.enter_context(tc.psum_pool(name="psum_h", bufs=3))
+        psum_o = stack.enter_context(tc.psum_pool(name="psum_o", bufs=2))
+
+        identity = const.tile([P, P], F32)
+        make_identity(nc, identity[:])
+
+        w1_in = const.tile([P, COMPS, D_IN], BF16)
+        for c in range(COMPS):
+            nc.scalar.dma_start(out=w1_in[:, c, :], in_=w1[c])
+
+        def load_chunk(n):
+            q_rows = q_pool.tile([P, COMPS, SUB_ROWS, D_IN], BF16, name="q_rows")
+            for c in range(COMPS):
+                rows = q[c][n * CHUNK : (n + 1) * CHUNK, :]
+                nc.sync.dma_start(out=q_rows[:, c, :, :], in_=rows.rearrange("(p t) k -> p t k", t=SUB_ROWS))
+            return q_rows
+
+        q_chunks = [load_chunk(0)]
+
+        w2_in = const.tile([P, COMPS, D_HID], BF16)
+        for c in range(COMPS):
+            nc.scalar.dma_start(out=w2_in[:, c, :], in_=w2[c])
+
+        b1_cols = const.tile([P, PACK], BF16)
+        for o in range(COMPS):
+            nc.gpsimd.dma_start(
+                out=b1_cols[o * QUADRANT : (o + 1) * QUADRANT, :],
+                in_=b1[o].rearrange("(i j) -> i j", j=PACK),
+            )
+        b2_rows = const.tile([P, COMPS, D_OUT], BF16)
+        for o in range(COMPS):
+            nc.gpsimd.dma_start(out=b2_rows[:, o, :], in_=b2[o].partition_broadcast(P))
+
+        for n in range(1, N_CHUNKS):
+            q_chunks.append(load_chunk(n))
+
+        w1_t = psum_t.tile([P, COMPS, D_HID], F32, tag="transposed")
+        for c in range(COMPS):
+            nc.tensor.transpose(w1_t[:, c, :], w1_in[:, c, :].bitcast(F32), identity[:])
+        w1_grouped = const.tile([P, PACK, L1_PASSES, P, PACK], BF16, align_bytes=64)
+        for o in range(COMPS):
+            for c in range(COMPS):
+                g, u = divmod(c, 2)
+                source = w1_t[:, o ^ c, :].bitcast(BF16).rearrange("p (i j e) -> p j i e", j=PACK, e=2)
+                target = w1_grouped[:, :, g, o * QUADRANT : (o + 1) * QUADRANT, 2 * u : 2 * u + 2]
+                if o % 2 == 0:
+                    nc.vector.tensor_scalar_mul(out=target, in0=source, scalar1=HAMILTON_SIGN[o][c])
+                else:
+                    nc.scalar.mul(out=target, in_=source, mul=HAMILTON_SIGN[o][c])
+        w1_codes = const.tile([P, PACK, L1_PASSES, P], U32, align_bytes=64)
+        w1_scales = const.tile([P, PACK, L1_PASSES, P], U8, align_bytes=64)
+        nc.vector.quantize_mx(
+            out=w1_codes[:].rearrange("p j g m -> p (j g m)").bitcast(FP8X4),
+            scales=w1_scales[:].rearrange("p j g m -> p (j g m)"),
+            in_=w1_grouped[:].rearrange("p j g m t -> p (j g m t)"),
+        )
+
+        def prepare_w2():
+            w2_rows = const.tile([P, COMPS, COMPS * D_HID], BF16)
+            for o in range(COMPS):
+                for c in range(COMPS):
+                    nc.vector.tensor_scalar_mul(
+                        out=w2_rows[:, o, c * D_HID : (c + 1) * D_HID],
+                        in0=w2_in[:, o ^ c, :],
+                        scalar1=HAMILTON_SIGN[o][c],
+                    )
+            w2_grouped = const.tile([P, COMPS * D_OUT * PACK], BF16, align_bytes=64)
+            for half in range(2):
+                w2_t = psum_t.tile([P, 2, 2, D_OUT], F32, tag="transposed")
+                for a in range(2):
+                    words = w2_rows[:, 2 * half + a, :].bitcast(F32).rearrange("f (p u) -> f u p", u=2)
+                    for u in range(2):
+                        nc.tensor.transpose(w2_t[:, a, u, :], words[:, u, :], identity[:])
+                columns = w2_grouped[:, half * 2 * D_OUT * PACK : (half + 1) * 2 * D_OUT * PACK]
+                nc.scalar.copy(out=pair_words(columns), in_=w2_t[:].rearrange("p a u r -> p a r u"))
+            w2_codes = const.tile([P, COMPS * D_OUT], U32, align_bytes=64)
+            w2_scales = const.tile([P, COMPS * D_OUT], U8, align_bytes=64)
+            nc.vector.quantize_mx(out=w2_codes[:].bitcast(FP8X4), scales=w2_scales[:], in_=w2_grouped[:])
+            return w2_codes, w2_scales
+
+        def transpose_and_quantise(q_rows):
+            q_grouped = work.tile([P, L1_PASSES, CHUNK * PACK], BF16, align_bytes=64)
+            q_codes = work.tile([P, L1_PASSES, CHUNK], U32, align_bytes=64)
+            q_scales = work.tile([P, L1_PASSES, CHUNK], U8, align_bytes=64)
+            for g in range(L1_PASSES):
+                for half in range(SUB_ROWS // 2):
+                    q_t = psum_t.tile([P, 2, 2, P], F32, tag="transposed")
+                    for a in range(2):
+                        for u in range(2):
+                            words = q_rows[:, 2 * g + u, 2 * half + a, :].bitcast(F32)
+                            nc.tensor.transpose(q_t[:, a, u, :], words, identity[:])
+                    columns = q_grouped[:, g, half * 2 * P * PACK : (half + 1) * 2 * P * PACK]
+                    nc.scalar.copy(out=pair_words(columns), in_=q_t[:].rearrange("p a u r -> p a r u"))
+                nc.vector.quantize_mx(
+                    out=q_codes[:, g, :].bitcast(FP8X4), scales=q_scales[:, g, :], in_=q_grouped[:, g, :]
+                )
+            return q_codes, q_scales
+
+        def layer_1(q_codes, q_scales):
+            h_tiles = work.tile([P, PACK, CHUNK], BF16)
+            for j in range(PACK):
+                h_acc = psum_h.tile([P, CHUNK], F32)
+                for g in range(L1_PASSES):
+                    nc.tensor.matmul_mx(
+                        out=h_acc[:],
+                        lhsT=w1_codes[:, j, g, :].bitcast(FP8X4),
+                        lhsT_scale=w1_scales[:, j, g, :],
+                        rhs=q_codes[:, g, :].bitcast(FP8X4),
+                        rhs_scale=q_scales[:, g, :],
+                        start=(g == 0),
+                        stop=(g == L1_PASSES - 1),
+                    )
+                nc.scalar.activation(out=h_tiles[:, j, :], in_=h_acc[:], func=RELU, bias=b1_cols[:, j : j + 1])
+            h_grouped = work.tile([P, CHUNK, PACK], BF16, align_bytes=64)
+            nc.vector.tensor_copy(
+                out=h_grouped[:].rearrange("p (c i) j -> p c j i", i=4),
+                in_=h_tiles[:].rearrange("p j (c i) -> p c j i", i=4),
+            )
+            h_codes = work.tile([P, CHUNK], U32, align_bytes=64)
+            h_scales = work.tile([P, CHUNK], U8, align_bytes=64)
+            nc.vector.quantize_mx(
+                out=h_codes[:].bitcast(FP8X4), scales=h_scales[:], in_=h_grouped[:].rearrange("p n j -> p (n j)")
+            )
+            return h_codes, h_scales
+
+        def layer_2(n, h_codes, h_scales, w2_codes, w2_scales):
+            out_rows = out_pool.tile([P, COMPS, SUB_ROWS, D_OUT], F32)
+            for t in range(SUB_ROWS):
+                out_acc = psum_o.tile([P, COMPS, D_OUT], F32)
+                nc.tensor.matmul_mx(
+                    out=out_acc[:].rearrange("p o f -> p (o f)"),
+                    lhsT=h_codes[:, t * P : (t + 1) * P].bitcast(FP8X4),
+                    lhsT_scale=h_scales[:, t * P : (t + 1) * P],
+                    rhs=w2_codes[:].bitcast(FP8X4),
+                    rhs_scale=w2_scales[:],
+                    start=True,
+                    stop=True,
+                )
+                nc.vector.tensor_tensor(out=out_rows[:, :, t, :], in0=out_acc[:], in1=b2_rows[:], op=ADD)
+            for o in range(COMPS):
+                rows = outs[o][n * CHUNK : (n + 1) * CHUNK, :]
+                nc.sync.dma_start(out=rows.rearrange("(p t) f -> p t f", t=SUB_ROWS), in_=out_rows[:, o, :, :])
+
+        q_mx = {0: transpose_and_quantise(q_chunks[0])}
+        w2_codes, w2_scales = prepare_w2()
+        h_mx = {}
+        for n in range(1, N_CHUNKS + 2):
+            if n < N_CHUNKS:
+                q_mx[n] = transpose_and_quantise(q_chunks[n])
+            if n - 1 < N_CHUNKS:
+                h_mx[n - 1] = layer_1(*q_mx[n - 1])
+            if n >= 2:
+                layer_2(n - 2, *h_mx[n - 2], w2_codes, w2_scales)

@@ -64,26 +64,32 @@ def tile_qmlp_t_kernel(
         psum_t = stack.enter_context(tc.psum_pool(name="psum_t", bufs=3))
         psum_h = stack.enter_context(tc.psum_pool(name="psum_h", bufs=3))
         psum_o = stack.enter_context(tc.psum_pool(name="psum_o", bufs=2))
+        stack.enter_context(tc.manual_schedule())
 
         identity = const.tile([P, P], F32)
         make_identity(nc, identity[:])
 
+        q_rows = {}
+
+        def load_chunk(n):
+            q_rows[n] = q_pool.tile([P, COMPS, SUB_ROWS, D_IN], BF16, name="q_rows")
+            for c in range(COMPS):
+                rows = q[c][n * CHUNK : (n + 1) * CHUNK, :]
+                nc.sync.dma_start(out=q_rows[n][:, c, :, :], in_=rows.rearrange("(p t) k -> p t k", t=SUB_ROWS))
+
         w1_in = const.tile([P, COMPS, D_IN], BF16)
         for c in range(COMPS):
             nc.scalar.dma_start(out=w1_in[:, c, :], in_=w1[c])
-
-        def load_chunk(n):
-            q_rows = q_pool.tile([P, COMPS, SUB_ROWS, D_IN], BF16, name="q_rows")
-            for c in range(COMPS):
-                rows = q[c][n * CHUNK : (n + 1) * CHUNK, :]
-                nc.sync.dma_start(out=q_rows[:, c, :, :], in_=rows.rearrange("(p t) k -> p t k", t=SUB_ROWS))
-            return q_rows
-
-        q_chunks = [load_chunk(0)]
-
+        warm = const.tile([P, 1], F32)
+        nc.vector.memset(warm[:], 0.0)
+        nc.scalar.activation(out=warm[:], in_=warm[:], func=RELU)
+        load_chunk(0)
+        load_chunk(1)
         w2_in = const.tile([P, COMPS, D_HID], BF16)
         for c in range(COMPS):
-            nc.scalar.dma_start(out=w2_in[:, c, :], in_=w2[c])
+            nc.sync.dma_start(out=w2_in[:, c, :], in_=w2[c])
+        for n in range(2, N_CHUNKS):
+            load_chunk(n)
 
         b1_cols = const.tile([P, PACK], BF16)
         for o in range(COMPS):
@@ -95,15 +101,12 @@ def tile_qmlp_t_kernel(
         for o in range(COMPS):
             nc.gpsimd.dma_start(out=b2_rows[:, o, :], in_=b2[o].partition_broadcast(P))
 
-        for n in range(1, N_CHUNKS):
-            q_chunks.append(load_chunk(n))
-
-        w1_t = psum_t.tile([P, COMPS, D_HID], F32, tag="transposed")
+        w1_t = psum_h.tile([P, COMPS, D_HID], F32, tag="h_acc")
         for c in range(COMPS):
             nc.tensor.transpose(w1_t[:, c, :], w1_in[:, c, :].bitcast(F32), identity[:])
         w1_grouped = const.tile([P, PACK, L1_PASSES, P, PACK], BF16, align_bytes=64)
-        for o in range(COMPS):
-            for c in range(COMPS):
+        for c in range(COMPS):
+            for o in range(COMPS):
                 g, u = divmod(c, 2)
                 source = w1_t[:, o ^ c, :].bitcast(BF16).rearrange("p (i j e) -> p j i e", j=PACK, e=2)
                 target = w1_grouped[:, :, g, o * QUADRANT : (o + 1) * QUADRANT, 2 * u : 2 * u + 2]
@@ -119,6 +122,9 @@ def tile_qmlp_t_kernel(
             in_=w1_grouped[:].rearrange("p j g m t -> p (j g m t)"),
         )
 
+        w2_codes = const.tile([P, COMPS * D_OUT], U32, align_bytes=64)
+        w2_scales = const.tile([P, COMPS * D_OUT], U8, align_bytes=64)
+
         def prepare_w2():
             w2_rows = const.tile([P, COMPS, COMPS * D_HID], BF16)
             for o in range(COMPS):
@@ -130,88 +136,126 @@ def tile_qmlp_t_kernel(
                     )
             w2_grouped = const.tile([P, COMPS * D_OUT * PACK], BF16, align_bytes=64)
             for half in range(2):
-                w2_t = psum_t.tile([P, 2, 2, D_OUT], F32, tag="transposed")
+                w2_t = psum_o.tile([P, 2, 2, D_OUT], F32, tag="out_acc")
                 for a in range(2):
                     words = w2_rows[:, 2 * half + a, :].bitcast(F32).rearrange("f (p u) -> f u p", u=2)
                     for u in range(2):
                         nc.tensor.transpose(w2_t[:, a, u, :], words[:, u, :], identity[:])
                 columns = w2_grouped[:, half * 2 * D_OUT * PACK : (half + 1) * 2 * D_OUT * PACK]
                 nc.scalar.copy(out=pair_words(columns), in_=w2_t[:].rearrange("p a u r -> p a r u"))
-            w2_codes = const.tile([P, COMPS * D_OUT], U32, align_bytes=64)
-            w2_scales = const.tile([P, COMPS * D_OUT], U8, align_bytes=64)
             nc.vector.quantize_mx(out=w2_codes[:].bitcast(FP8X4), scales=w2_scales[:], in_=w2_grouped[:])
-            return w2_codes, w2_scales
 
-        def transpose_and_quantise(q_rows):
-            q_grouped = work.tile([P, L1_PASSES, CHUNK * PACK], BF16, align_bytes=64)
-            q_codes = work.tile([P, L1_PASSES, CHUNK], U32, align_bytes=64)
-            q_scales = work.tile([P, L1_PASSES, CHUNK], U8, align_bytes=64)
+        q_grouped, q_codes, q_scales = {}, {}, {}
+        h_tiles, h_grouped, h_codes, h_scales = {}, {}, {}, {}
+        out_rows = {}
+
+        def is_chunk(n):
+            return 0 <= n < N_CHUNKS
+
+        def transpose_q(n):
+            if not is_chunk(n):
+                return
+            q_grouped[n] = work.tile([P, L1_PASSES, CHUNK * PACK], BF16, name="q_grouped", align_bytes=64)
             for g in range(L1_PASSES):
                 for half in range(SUB_ROWS // 2):
-                    q_t = psum_t.tile([P, 2, 2, P], F32, tag="transposed")
+                    q_t = psum_t.tile([P, 2, 2, P], F32)
                     for a in range(2):
                         for u in range(2):
-                            words = q_rows[:, 2 * g + u, 2 * half + a, :].bitcast(F32)
+                            words = q_rows[n][:, 2 * g + u, 2 * half + a, :].bitcast(F32)
                             nc.tensor.transpose(q_t[:, a, u, :], words, identity[:])
-                    columns = q_grouped[:, g, half * 2 * P * PACK : (half + 1) * 2 * P * PACK]
+                    columns = q_grouped[n][:, g, half * 2 * P * PACK : (half + 1) * 2 * P * PACK]
                     nc.scalar.copy(out=pair_words(columns), in_=q_t[:].rearrange("p a u r -> p a r u"))
-                nc.vector.quantize_mx(
-                    out=q_codes[:, g, :].bitcast(FP8X4), scales=q_scales[:, g, :], in_=q_grouped[:, g, :]
-                )
-            return q_codes, q_scales
 
-        def layer_1(q_codes, q_scales):
-            h_tiles = work.tile([P, PACK, CHUNK], BF16)
-            for j in range(PACK):
-                h_acc = psum_h.tile([P, CHUNK], F32)
-                for g in range(L1_PASSES):
-                    nc.tensor.matmul_mx(
-                        out=h_acc[:],
-                        lhsT=w1_codes[:, j, g, :].bitcast(FP8X4),
-                        lhsT_scale=w1_scales[:, j, g, :],
-                        rhs=q_codes[:, g, :].bitcast(FP8X4),
-                        rhs_scale=q_scales[:, g, :],
-                        start=(g == 0),
-                        stop=(g == L1_PASSES - 1),
-                    )
-                nc.scalar.activation(out=h_tiles[:, j, :], in_=h_acc[:], func=RELU, bias=b1_cols[:, j : j + 1])
-            h_grouped = work.tile([P, CHUNK, PACK], BF16, align_bytes=64)
-            nc.vector.tensor_copy(
-                out=h_grouped[:].rearrange("p (c i) j -> p c j i", i=4),
-                in_=h_tiles[:].rearrange("p j (c i) -> p c j i", i=4),
-            )
-            h_codes = work.tile([P, CHUNK], U32, align_bytes=64)
-            h_scales = work.tile([P, CHUNK], U8, align_bytes=64)
+        def quantise_q(n, g):
+            if not is_chunk(n):
+                return
+            if g == 0:
+                q_codes[n] = work.tile([P, L1_PASSES, CHUNK], U32, name="q_codes", align_bytes=64)
+                q_scales[n] = work.tile([P, L1_PASSES, CHUNK], U8, name="q_scales", align_bytes=64)
             nc.vector.quantize_mx(
-                out=h_codes[:].bitcast(FP8X4), scales=h_scales[:], in_=h_grouped[:].rearrange("p n j -> p (n j)")
+                out=q_codes[n][:, g, :].bitcast(FP8X4), scales=q_scales[n][:, g, :], in_=q_grouped[n][:, g, :]
             )
-            return h_codes, h_scales
 
-        def layer_2(n, h_codes, h_scales, w2_codes, w2_scales):
-            out_rows = out_pool.tile([P, COMPS, SUB_ROWS, D_OUT], F32)
-            for t in range(SUB_ROWS):
-                out_acc = psum_o.tile([P, COMPS, D_OUT], F32)
+        def layer_1_tile(n, j):
+            if not is_chunk(n):
+                return
+            if j == 0:
+                h_tiles[n] = work.tile([P, PACK, CHUNK], BF16, name="h_tiles")
+            h_acc = psum_h.tile([P, CHUNK], F32)
+            for g in range(L1_PASSES):
                 nc.tensor.matmul_mx(
-                    out=out_acc[:].rearrange("p o f -> p (o f)"),
-                    lhsT=h_codes[:, t * P : (t + 1) * P].bitcast(FP8X4),
-                    lhsT_scale=h_scales[:, t * P : (t + 1) * P],
-                    rhs=w2_codes[:].bitcast(FP8X4),
-                    rhs_scale=w2_scales[:],
-                    start=True,
-                    stop=True,
+                    out=h_acc[:],
+                    lhsT=w1_codes[:, j, g, :].bitcast(FP8X4),
+                    lhsT_scale=w1_scales[:, j, g, :],
+                    rhs=q_codes[n][:, g, :].bitcast(FP8X4),
+                    rhs_scale=q_scales[n][:, g, :],
+                    start=(g == 0),
+                    stop=(g == L1_PASSES - 1),
                 )
-                nc.vector.tensor_tensor(out=out_rows[:, :, t, :], in0=out_acc[:], in1=b2_rows[:], op=ADD)
+            nc.scalar.activation(out=h_tiles[n][:, j, :], in_=h_acc[:], func=RELU, bias=b1_cols[:, j : j + 1])
+
+        def regroup_h(n):
+            if not is_chunk(n):
+                return
+            h_grouped[n] = work.tile([P, CHUNK, PACK], BF16, name="h_grouped", align_bytes=64)
+            nc.vector.tensor_copy(
+                out=h_grouped[n][:].rearrange("p (c i) j -> p c j i", i=4),
+                in_=h_tiles[n][:].rearrange("p j (c i) -> p c j i", i=4),
+            )
+
+        def quantise_h(n):
+            if not is_chunk(n):
+                return
+            h_codes[n] = work.tile([P, CHUNK], U32, name="h_codes", align_bytes=64)
+            h_scales[n] = work.tile([P, CHUNK], U8, name="h_scales", align_bytes=64)
+            nc.vector.quantize_mx(
+                out=h_codes[n][:].bitcast(FP8X4),
+                scales=h_scales[n][:],
+                in_=h_grouped[n][:].rearrange("p n j -> p (n j)"),
+            )
+
+        def layer_2_block(n, t):
+            if not is_chunk(n):
+                return
+            if t == 0:
+                out_rows[n] = out_pool.tile([P, COMPS, SUB_ROWS, D_OUT], F32, name="out_rows")
+            out_acc = psum_o.tile([P, COMPS, D_OUT], F32)
+            nc.tensor.matmul_mx(
+                out=out_acc[:].rearrange("p o f -> p (o f)"),
+                lhsT=h_codes[n][:, t * P : (t + 1) * P].bitcast(FP8X4),
+                lhsT_scale=h_scales[n][:, t * P : (t + 1) * P],
+                rhs=w2_codes[:].bitcast(FP8X4),
+                rhs_scale=w2_scales[:],
+                start=True,
+                stop=True,
+            )
+            nc.vector.tensor_tensor(out=out_rows[n][:, :, t, :], in0=out_acc[:], in1=b2_rows[:], op=ADD)
+
+        def store(n):
+            if not is_chunk(n):
+                return
             for o in range(COMPS):
                 rows = outs[o][n * CHUNK : (n + 1) * CHUNK, :]
-                nc.sync.dma_start(out=rows.rearrange("(p t) f -> p t f", t=SUB_ROWS), in_=out_rows[:, o, :, :])
+                nc.sync.dma_start(out=rows.rearrange("(p t) f -> p t f", t=SUB_ROWS), in_=out_rows[n][:, o, :, :])
 
-        q_mx = {0: transpose_and_quantise(q_chunks[0])}
-        w2_codes, w2_scales = prepare_w2()
-        h_mx = {}
+        def run_round(n):
+            regroup_h(n - 1)
+            transpose_q(n + 1)
+            quantise_q(n + 1, 0)
+            layer_1_tile(n, 0)
+            layer_2_block(n - 2, 0)
+            quantise_h(n - 1)
+            layer_1_tile(n, 1)
+            layer_2_block(n - 2, 1)
+            quantise_q(n + 1, 1)
+            layer_1_tile(n, 2)
+            layer_2_block(n - 2, 2)
+            layer_1_tile(n, 3)
+            layer_2_block(n - 2, 3)
+            store(n - 2)
+
+        run_round(-1)
+        run_round(0)
+        prepare_w2()
         for n in range(1, N_CHUNKS + 2):
-            if n < N_CHUNKS:
-                q_mx[n] = transpose_and_quantise(q_chunks[n])
-            if n - 1 < N_CHUNKS:
-                h_mx[n - 1] = layer_1(*q_mx[n - 1])
-            if n >= 2:
-                layer_2(n - 2, *h_mx[n - 2], w2_codes, w2_scales)
+            run_round(n)

@@ -61,9 +61,8 @@ def tile_qmlp_t_kernel(
         q_pool = stack.enter_context(tc.tile_pool(name="q_rows", bufs=N_CHUNKS))
         work = stack.enter_context(tc.tile_pool(name="work", bufs=2))
         out_pool = stack.enter_context(tc.tile_pool(name="out_rows", bufs=3))
-        psum_t = stack.enter_context(tc.psum_pool(name="psum_t", bufs=3))
-        psum_h = stack.enter_context(tc.psum_pool(name="psum_h", bufs=3))
-        psum_o = stack.enter_context(tc.psum_pool(name="psum_o", bufs=2))
+        psum_s = stack.enter_context(tc.psum_pool(name="psum_s", bufs=5))
+        psum_v = stack.enter_context(tc.psum_pool(name="psum_v", bufs=3))
         stack.enter_context(tc.manual_schedule())
 
         identity = const.tile([P, P], F32)
@@ -101,7 +100,7 @@ def tile_qmlp_t_kernel(
         for o in range(COMPS):
             nc.gpsimd.dma_start(out=b2_rows[:, o, :], in_=b2[o].partition_broadcast(P))
 
-        w1_t = psum_h.tile([P, COMPS, D_HID], F32, tag="h_acc")
+        w1_t = psum_s.tile([P, COMPS, D_HID], F32, tag="for_scalar")
         for c in range(COMPS):
             nc.tensor.transpose(w1_t[:, c, :], w1_in[:, c, :].bitcast(F32), identity[:])
         w1_grouped = const.tile([P, PACK, L1_PASSES, P, PACK], BF16, align_bytes=64)
@@ -136,7 +135,7 @@ def tile_qmlp_t_kernel(
                     )
             w2_grouped = const.tile([P, COMPS * D_OUT * PACK], BF16, align_bytes=64)
             for half in range(2):
-                w2_t = psum_o.tile([P, 2, 2, D_OUT], F32, tag="out_acc")
+                w2_t = psum_v.tile([P, 2, 2, D_OUT], F32, tag="for_vector")
                 for a in range(2):
                     words = w2_rows[:, 2 * half + a, :].bitcast(F32).rearrange("f (p u) -> f u p", u=2)
                     for u in range(2):
@@ -158,7 +157,7 @@ def tile_qmlp_t_kernel(
             q_grouped[n] = work.tile([P, L1_PASSES, CHUNK * PACK], BF16, name="q_grouped", align_bytes=64)
             for g in range(L1_PASSES):
                 for half in range(SUB_ROWS // 2):
-                    q_t = psum_t.tile([P, 2, 2, P], F32)
+                    q_t = psum_s.tile([P, 2, 2, P], F32, tag="for_scalar")
                     for a in range(2):
                         for u in range(2):
                             words = q_rows[n][:, 2 * g + u, 2 * half + a, :].bitcast(F32)
@@ -181,7 +180,7 @@ def tile_qmlp_t_kernel(
                 return
             if j == 0:
                 h_tiles[n] = work.tile([P, PACK, CHUNK], BF16, name="h_tiles")
-            h_acc = psum_h.tile([P, CHUNK], F32)
+            h_acc = psum_s.tile([P, CHUNK], F32, tag="for_scalar")
             for g in range(L1_PASSES):
                 nc.tensor.matmul_mx(
                     out=h_acc[:],
@@ -219,7 +218,7 @@ def tile_qmlp_t_kernel(
                 return
             if t == 0:
                 out_rows[n] = out_pool.tile([P, COMPS, SUB_ROWS, D_OUT], F32, name="out_rows")
-            out_acc = psum_o.tile([P, COMPS, D_OUT], F32)
+            out_acc = psum_v.tile([P, COMPS, D_OUT], F32, tag="for_vector")
             nc.tensor.matmul_mx(
                 out=out_acc[:].rearrange("p o f -> p (o f)"),
                 lhsT=h_codes[n][:, t * P : (t + 1) * P].bitcast(FP8X4),

@@ -10,6 +10,7 @@ U8 = mybir.dt.uint8
 FP8X4 = mybir.dt.float8_e4m3fn_x4
 RELU = mybir.ActivationFunctionType.Relu
 ADD = mybir.AluOpType.add
+MULT = mybir.AluOpType.mult
 
 P = 128
 PACK = 4
@@ -197,9 +198,13 @@ def tile_qmlp_t_kernel(
             if not is_chunk(n):
                 return
             h_grouped[n] = work.tile([P, CHUNK, PACK], BF16, name="h_grouped", align_bytes=64)
-            nc.vector.tensor_copy(
-                out=h_grouped[n][:].rearrange("p (c i) j -> p c j i", i=4),
-                in_=h_tiles[n][:].rearrange("p j (c i) -> p c j i", i=4),
+            nc.gpsimd.tensor_scalar(
+                out=h_grouped[n][:],
+                in0=h_tiles[n][:].rearrange("p j n -> p n j"),
+                scalar1=1.0,
+                scalar2=0.0,
+                op0=MULT,
+                op1=ADD,
             )
 
         def quantise_h(n):

@@ -10,7 +10,6 @@ U8 = mybir.dt.uint8
 FP8X4 = mybir.dt.float8_e4m3fn_x4
 RELU = mybir.ActivationFunctionType.Relu
 ADD = mybir.AluOpType.add
-MULT = mybir.AluOpType.mult
 
 P = 128
 PACK = 4
@@ -26,12 +25,19 @@ CHUNK = P * SUB_ROWS
 N_CHUNKS = ROWS // CHUNK
 QUADRANT = P // COMPS
 
+R, I, J, K = range(COMPS)
 HAMILTON_SIGN = (
     (1.0, -1.0, -1.0, -1.0),
     (1.0, 1.0, 1.0, -1.0),
     (1.0, -1.0, 1.0, 1.0),
     (1.0, 1.0, -1.0, 1.0),
 )
+W1_PLANES = (
+    ((1.0, R), (1.0, I), (-1.0, I), (1.0, R)),
+    ((1.0, K), (1.0, J), (-1.0, J), (-1.0, K)),
+)
+LAYER_2_LAG = 2
+SCALAR_COLUMNS = 192
 
 FLOPS = 2 * ROWS * (COMPS * D_IN) * (COMPS * D_HID) + 2 * ROWS * (COMPS * D_HID) * (COMPS * D_OUT)
 
@@ -77,9 +83,9 @@ def tile_qmlp_t_kernel(
                 rows = q[c][n * CHUNK : (n + 1) * CHUNK, :]
                 nc.sync.dma_start(out=q_rows[n][:, c, :, :], in_=rows.rearrange("(p t) k -> p t k", t=SUB_ROWS))
 
-        w1_in = const.tile([P, COMPS, D_IN], BF16)
+        w1_plus = const.tile([P, COMPS, D_IN], BF16)
         for c in range(COMPS):
-            nc.scalar.dma_start(out=w1_in[:, c, :], in_=w1[c])
+            nc.sync.dma_start(out=w1_plus[:, c, :], in_=w1[c])
         warm = const.tile([P, 1], F32)
         nc.vector.memset(warm[:], 0.0)
         nc.scalar.activation(out=warm[:], in_=warm[:], func=RELU)
@@ -101,32 +107,45 @@ def tile_qmlp_t_kernel(
         for o in range(COMPS):
             nc.gpsimd.dma_start(out=b2_rows[:, o, :], in_=b2[o].partition_broadcast(P))
 
-        w1_t = psum_s.tile([P, COMPS, D_HID], F32, tag="for_scalar")
-        for c in range(COMPS):
-            nc.tensor.transpose(w1_t[:, c, :], w1_in[:, c, :].bitcast(F32), identity[:])
-        w1_grouped = const.tile([P, PACK, L1_PASSES, P, PACK], BF16, align_bytes=64)
-        for c in range(COMPS):
+        w1_minus = const.tile([P, COMPS, D_IN], BF16)
+        nc.vector.tensor_scalar_mul(out=w1_minus[:, I:, :], in0=w1_plus[:, I:, :], scalar1=-1.0)
+        w1_signed = {1.0: w1_plus, -1.0: w1_minus}
+        w1_t = [psum_s.tile([P, COMPS, D_HID], F32, name="w1_t", tag="for_scalar") for planes in W1_PLANES]
+        for wanted in (1.0, -1.0):
+            for b, planes in enumerate(W1_PLANES):
+                for x, (sign, c) in enumerate(planes):
+                    if sign == wanted:
+                        nc.tensor.transpose(w1_t[b][:, x, :], w1_signed[sign][:, c, :].bitcast(F32), identity[:])
+        w1_words = const.tile([P, L1_PASSES, PACK, P, 2], F32, align_bytes=64)
+        w1_codes = const.tile([P, L1_PASSES, PACK, P], U32, align_bytes=64)
+        w1_scales = const.tile([P, L1_PASSES, PACK, P], U8, align_bytes=64)
+        for g in range(L1_PASSES):
             for o in range(COMPS):
-                g, u = divmod(c, 2)
-                source = w1_t[:, o ^ c, :].bitcast(BF16).rearrange("p (i j e) -> p j i e", j=PACK, e=2)
-                target = w1_grouped[:, :, g, o * QUADRANT : (o + 1) * QUADRANT, 2 * u : 2 * u + 2]
+                first = (HAMILTON_SIGN[o][2 * g], o ^ (2 * g))
+                second = (HAMILTON_SIGN[o][2 * g + 1], o ^ (2 * g + 1))
+                b = first[1] // 2
+                x = W1_PLANES[b].index(first)
+                y = COMPS - 1 - W1_PLANES[b][::-1].index(second)
+                assert x < y
+                source = w1_t[b][:, x : y + 1 : y - x, :].rearrange("p u (i j) -> p j i u", j=PACK)
+                target = w1_words[:, g, :, o * QUADRANT : (o + 1) * QUADRANT, :]
                 if o % 2 == 0:
-                    nc.vector.tensor_scalar_mul(out=target, in0=source, scalar1=HAMILTON_SIGN[o][c])
+                    nc.vector.tensor_copy(out=target, in_=source)
                 else:
-                    nc.scalar.mul(out=target, in_=source, mul=HAMILTON_SIGN[o][c])
-        w1_codes = const.tile([P, PACK, L1_PASSES, P], U32, align_bytes=64)
-        w1_scales = const.tile([P, PACK, L1_PASSES, P], U8, align_bytes=64)
-        nc.vector.quantize_mx(
-            out=w1_codes[:].rearrange("p j g m -> p (j g m)").bitcast(FP8X4),
-            scales=w1_scales[:].rearrange("p j g m -> p (j g m)"),
-            in_=w1_grouped[:].rearrange("p j g m t -> p (j g m t)"),
-        )
+                    nc.scalar.copy(out=target, in_=source)
+        for g in range(L1_PASSES):
+            nc.vector.quantize_mx(
+                out=w1_codes[:, g, :, :].rearrange("p j m -> p (j m)").bitcast(FP8X4),
+                scales=w1_scales[:, g, :, :].rearrange("p j m -> p (j m)"),
+                in_=w1_words[:, g, :, :, :].rearrange("p j m u -> p (j m u)").bitcast(BF16),
+            )
 
+        w2_rows = const.tile([P, COMPS, COMPS * D_HID], BF16)
+        w2_grouped = const.tile([P, COMPS * D_OUT * PACK], BF16, align_bytes=64)
         w2_codes = const.tile([P, COMPS * D_OUT], U32, align_bytes=64)
         w2_scales = const.tile([P, COMPS * D_OUT], U8, align_bytes=64)
 
-        def prepare_w2():
-            w2_rows = const.tile([P, COMPS, COMPS * D_HID], BF16)
+        def sign_w2():
             for o in range(COMPS):
                 for c in range(COMPS):
                     nc.vector.tensor_scalar_mul(
@@ -134,7 +153,8 @@ def tile_qmlp_t_kernel(
                         in0=w2_in[:, o ^ c, :],
                         scalar1=HAMILTON_SIGN[o][c],
                     )
-            w2_grouped = const.tile([P, COMPS * D_OUT * PACK], BF16, align_bytes=64)
+
+        def transpose_w2():
             for half in range(2):
                 w2_t = psum_v.tile([P, 2, 2, D_OUT], F32, tag="for_vector")
                 for a in range(2):
@@ -143,6 +163,8 @@ def tile_qmlp_t_kernel(
                         nc.tensor.transpose(w2_t[:, a, u, :], words[:, u, :], identity[:])
                 columns = w2_grouped[:, half * 2 * D_OUT * PACK : (half + 1) * 2 * D_OUT * PACK]
                 nc.scalar.copy(out=pair_words(columns), in_=w2_t[:].rearrange("p a u r -> p a r u"))
+
+        def quantise_w2():
             nc.vector.quantize_mx(out=w2_codes[:].bitcast(FP8X4), scales=w2_scales[:], in_=w2_grouped[:])
 
         q_grouped, q_codes, q_scales = {}, {}, {}
@@ -185,8 +207,8 @@ def tile_qmlp_t_kernel(
             for g in range(L1_PASSES):
                 nc.tensor.matmul_mx(
                     out=h_acc[:],
-                    lhsT=w1_codes[:, j, g, :].bitcast(FP8X4),
-                    lhsT_scale=w1_scales[:, j, g, :],
+                    lhsT=w1_codes[:, g, j, :].bitcast(FP8X4),
+                    lhsT_scale=w1_scales[:, g, j, :],
                     rhs=q_codes[n][:, g, :].bitcast(FP8X4),
                     rhs_scale=q_scales[n][:, g, :],
                     start=(g == 0),
@@ -198,14 +220,12 @@ def tile_qmlp_t_kernel(
             if not is_chunk(n):
                 return
             h_grouped[n] = work.tile([P, CHUNK, PACK], BF16, name="h_grouped", align_bytes=64)
-            nc.gpsimd.tensor_scalar(
-                out=h_grouped[n][:],
-                in0=h_tiles[n][:].rearrange("p j n -> p n j"),
-                scalar1=1.0,
-                scalar2=0.0,
-                op0=MULT,
-                op1=ADD,
-            )
+            target = h_grouped[n][:].rearrange("p (c i) j -> p c j i", i=4)
+            source = h_tiles[n][:].rearrange("p j (c i) -> p c j i", i=4)
+            split = SCALAR_COLUMNS // 4 if n >= LAYER_2_LAG else 0
+            if split > 0:
+                nc.scalar.copy(out=target[:, :split], in_=source[:, :split])
+            nc.vector.tensor_copy(out=target[:, split:], in_=source[:, split:])
 
         def quantise_h(n):
             if not is_chunk(n):
@@ -247,19 +267,22 @@ def tile_qmlp_t_kernel(
             transpose_q(n + 1)
             quantise_q(n + 1, 0)
             layer_1_tile(n, 0)
-            layer_2_block(n - 2, 0)
+            layer_2_block(n - LAYER_2_LAG, 0)
             quantise_h(n - 1)
             layer_1_tile(n, 1)
-            layer_2_block(n - 2, 1)
+            layer_2_block(n - LAYER_2_LAG, 1)
             quantise_q(n + 1, 1)
             layer_1_tile(n, 2)
-            layer_2_block(n - 2, 2)
+            layer_2_block(n - LAYER_2_LAG, 2)
             layer_1_tile(n, 3)
-            layer_2_block(n - 2, 3)
-            store(n - 2)
+            layer_2_block(n - LAYER_2_LAG, 3)
+            store(n - LAYER_2_LAG)
 
         run_round(-1)
+        sign_w2()
         run_round(0)
-        prepare_w2()
-        for n in range(1, N_CHUNKS + 2):
+        transpose_w2()
+        run_round(1)
+        quantise_w2()
+        for n in range(LAYER_2_LAG, N_CHUNKS + LAYER_2_LAG):
             run_round(n)

@@ -162,7 +162,7 @@ def tile_qmlp_t_kernel(
                     for u in range(2):
                         nc.tensor.transpose(w2_t[:, a, u, :], words[:, u, :], identity[:])
                 columns = w2_grouped[:, half * 2 * D_OUT * PACK : (half + 1) * 2 * D_OUT * PACK]
-                nc.scalar.copy(out=pair_words(columns), in_=w2_t[:].rearrange("p a u r -> p a r u"))
+                nc.vector.tensor_copy(out=pair_words(columns), in_=w2_t[:].rearrange("p a u r -> p a r u"))
 
         def quantise_w2():
             nc.vector.quantize_mx(out=w2_codes[:].bitcast(FP8X4), scales=w2_scales[:], in_=w2_grouped[:])
@@ -254,13 +254,15 @@ def tile_qmlp_t_kernel(
                 stop=True,
             )
             nc.vector.tensor_tensor(out=out_rows[n][:, :, t, :], in0=out_acc[:], in1=b2_rows[:], op=ADD)
+            if n == N_CHUNKS - 1:
+                store(n, t, t + 1)
+            elif t == SUB_ROWS - 1:
+                store(n, 0, SUB_ROWS)
 
-        def store(n):
-            if not is_chunk(n):
-                return
+        def store(n, t_from, t_to):
             for o in range(COMPS):
-                rows = outs[o][n * CHUNK : (n + 1) * CHUNK, :]
-                nc.sync.dma_start(out=rows.rearrange("(p t) f -> p t f", t=SUB_ROWS), in_=out_rows[n][:, o, :, :])
+                rows = outs[o][n * CHUNK : (n + 1) * CHUNK, :].rearrange("(p t) f -> p t f", t=SUB_ROWS)
+                nc.sync.dma_start(out=rows[:, t_from:t_to, :], in_=out_rows[n][:, o, t_from:t_to, :])
 
         def run_round(n):
             regroup_h(n - 1)
@@ -276,7 +278,6 @@ def tile_qmlp_t_kernel(
             layer_2_block(n - LAYER_2_LAG, 2)
             layer_1_tile(n, 3)
             layer_2_block(n - LAYER_2_LAG, 3)
-            store(n - LAYER_2_LAG)
 
         run_round(-1)
         sign_w2()

@@ -13,17 +13,18 @@ ADD = mybir.AluOpType.add
 
 P = 128
 PACK = 4
+PAIRS = 2
 COMPS = 4
 ROWS = 4096
 D_IN = 256
 D_HID = 128
 D_OUT = 128
-IN_WORDS = D_IN // 2
 L1_PASSES = COMPS * D_IN // (P * PACK)
 SUB_ROWS = 4
 CHUNK = P * SUB_ROWS
 N_CHUNKS = ROWS // CHUNK
 QUADRANT = P // COMPS
+BANK_GROUPS = 2
 
 R, I, J, K = range(COMPS)
 HAMILTON_SIGN = (
@@ -38,12 +39,13 @@ W1_PLANES = (
 )
 LAYER_2_LAG = 2
 SCALAR_COLUMNS = 192
+COLUMN_RUN = 4
 
 FLOPS = 2 * ROWS * (COMPS * D_IN) * (COMPS * D_HID) + 2 * ROWS * (COMPS * D_HID) * (COMPS * D_OUT)
 
 
-def pair_words(grouped_bf16):
-    return grouped_bf16.bitcast(F32).rearrange("p (a r u) -> p a r u", a=2, u=2)
+def as_pairs(values):
+    return values.bitcast(F32).rearrange("p (a r u) -> p a r u", a=BANK_GROUPS, u=PAIRS)
 
 
 def tile_qmlp_t_kernel(
@@ -94,7 +96,12 @@ def tile_qmlp_t_kernel(
         w2_in = const.tile([P, COMPS, D_HID], BF16)
         for c in range(COMPS):
             nc.sync.dma_start(out=w2_in[:, c, :], in_=w2[c])
-        for n in range(2, N_CHUNKS):
+        load_chunk(2)
+        load_chunk(3)
+        b2_rows = const.tile([P, COMPS, D_OUT], BF16)
+        for o in range(COMPS):
+            nc.sync.dma_start(out=b2_rows[:, o, :], in_=b2[o].partition_broadcast(P))
+        for n in range(4, N_CHUNKS):
             load_chunk(n)
 
         b1_cols = const.tile([P, PACK], BF16)
@@ -103,9 +110,6 @@ def tile_qmlp_t_kernel(
                 out=b1_cols[o * QUADRANT : (o + 1) * QUADRANT, :],
                 in_=b1[o].rearrange("(i j) -> i j", j=PACK),
             )
-        b2_rows = const.tile([P, COMPS, D_OUT], BF16)
-        for o in range(COMPS):
-            nc.gpsimd.dma_start(out=b2_rows[:, o, :], in_=b2[o].partition_broadcast(P))
 
         w1_minus = const.tile([P, COMPS, D_IN], BF16)
         nc.vector.tensor_scalar_mul(out=w1_minus[:, I:, :], in0=w1_plus[:, I:, :], scalar1=-1.0)
@@ -116,14 +120,14 @@ def tile_qmlp_t_kernel(
                 for x, (sign, c) in enumerate(planes):
                     if sign == wanted:
                         nc.tensor.transpose(w1_t[b][:, x, :], w1_signed[sign][:, c, :].bitcast(F32), identity[:])
-        w1_words = const.tile([P, L1_PASSES, PACK, P, 2], F32, align_bytes=64)
+        w1_words = const.tile([P, L1_PASSES, PACK, P, PAIRS], F32, align_bytes=64)
         w1_codes = const.tile([P, L1_PASSES, PACK, P], U32, align_bytes=64)
         w1_scales = const.tile([P, L1_PASSES, PACK, P], U8, align_bytes=64)
         for g in range(L1_PASSES):
             for o in range(COMPS):
-                first = (HAMILTON_SIGN[o][2 * g], o ^ (2 * g))
-                second = (HAMILTON_SIGN[o][2 * g + 1], o ^ (2 * g + 1))
-                b = first[1] // 2
+                first = (HAMILTON_SIGN[o][PAIRS * g], o ^ (PAIRS * g))
+                second = (HAMILTON_SIGN[o][PAIRS * g + 1], o ^ (PAIRS * g + 1))
+                b = first[1] // PAIRS
                 x = W1_PLANES[b].index(first)
                 y = COMPS - 1 - W1_PLANES[b][::-1].index(second)
                 assert x < y
@@ -155,14 +159,17 @@ def tile_qmlp_t_kernel(
                     )
 
         def transpose_w2():
-            for half in range(2):
-                w2_t = psum_v.tile([P, 2, 2, D_OUT], F32, tag="for_vector")
-                for a in range(2):
-                    words = w2_rows[:, 2 * half + a, :].bitcast(F32).rearrange("f (p u) -> f u p", u=2)
-                    for u in range(2):
-                        nc.tensor.transpose(w2_t[:, a, u, :], words[:, u, :], identity[:])
-                columns = w2_grouped[:, half * 2 * D_OUT * PACK : (half + 1) * 2 * D_OUT * PACK]
-                nc.vector.tensor_copy(out=pair_words(columns), in_=w2_t[:].rearrange("p a u r -> p a r u"))
+            for half in range(COMPS // BANK_GROUPS):
+                w2_t = psum_v.tile([P, BANK_GROUPS, PAIRS, D_OUT], F32, tag="for_vector")
+                for a in range(BANK_GROUPS):
+                    pairs = w2_rows[:, BANK_GROUPS * half + a, :].bitcast(F32).rearrange("f (p u) -> f u p", u=PAIRS)
+                    for u in range(PAIRS):
+                        nc.tensor.transpose(w2_t[:, a, u, :], pairs[:, u, :], identity[:])
+                width = BANK_GROUPS * D_OUT * PACK
+                nc.scalar.copy(
+                    out=as_pairs(w2_grouped[:, half * width : (half + 1) * width]),
+                    in_=w2_t[:].rearrange("p a u r -> p a r u"),
+                )
 
         def quantise_w2():
             nc.vector.quantize_mx(out=w2_codes[:].bitcast(FP8X4), scales=w2_scales[:], in_=w2_grouped[:])
@@ -179,14 +186,17 @@ def tile_qmlp_t_kernel(
                 return
             q_grouped[n] = work.tile([P, L1_PASSES, CHUNK * PACK], BF16, name="q_grouped", align_bytes=64)
             for g in range(L1_PASSES):
-                for half in range(SUB_ROWS // 2):
-                    q_t = psum_s.tile([P, 2, 2, P], F32, tag="for_scalar")
-                    for a in range(2):
-                        for u in range(2):
-                            words = q_rows[n][:, 2 * g + u, 2 * half + a, :].bitcast(F32)
-                            nc.tensor.transpose(q_t[:, a, u, :], words, identity[:])
-                    columns = q_grouped[n][:, g, half * 2 * P * PACK : (half + 1) * 2 * P * PACK]
-                    nc.scalar.copy(out=pair_words(columns), in_=q_t[:].rearrange("p a u r -> p a r u"))
+                for half in range(SUB_ROWS // BANK_GROUPS):
+                    q_t = psum_s.tile([P, BANK_GROUPS, PAIRS, P], F32, tag="for_scalar")
+                    for a in range(BANK_GROUPS):
+                        for u in range(PAIRS):
+                            pairs = q_rows[n][:, PAIRS * g + u, BANK_GROUPS * half + a, :].bitcast(F32)
+                            nc.tensor.transpose(q_t[:, a, u, :], pairs, identity[:])
+                    width = BANK_GROUPS * P * PACK
+                    nc.scalar.copy(
+                        out=as_pairs(q_grouped[n][:, g, half * width : (half + 1) * width]),
+                        in_=q_t[:].rearrange("p a u r -> p a r u"),
+                    )
 
         def quantise_q(n, g):
             if not is_chunk(n):
@@ -220,9 +230,9 @@ def tile_qmlp_t_kernel(
             if not is_chunk(n):
                 return
             h_grouped[n] = work.tile([P, CHUNK, PACK], BF16, name="h_grouped", align_bytes=64)
-            target = h_grouped[n][:].rearrange("p (c i) j -> p c j i", i=4)
-            source = h_tiles[n][:].rearrange("p j (c i) -> p c j i", i=4)
-            split = SCALAR_COLUMNS // 4 if n >= LAYER_2_LAG else 0
+            target = h_grouped[n][:].rearrange("p (c i) j -> p c j i", i=COLUMN_RUN)
+            source = h_tiles[n][:].rearrange("p j (c i) -> p c j i", i=COLUMN_RUN)
+            split = SCALAR_COLUMNS // COLUMN_RUN if n >= LAYER_2_LAG else 0
             if split > 0:
                 nc.scalar.copy(out=target[:, :split], in_=source[:, :split])
             nc.vector.tensor_copy(out=target[:, split:], in_=source[:, split:])
@@ -238,7 +248,7 @@ def tile_qmlp_t_kernel(
                 in_=h_grouped[n][:].rearrange("p n j -> p (n j)"),
             )
 
-        def layer_2_block(n, t):
+        def layer_2_sub_row(n, t):
             if not is_chunk(n):
                 return
             if t == 0:
@@ -254,30 +264,29 @@ def tile_qmlp_t_kernel(
                 stop=True,
             )
             nc.vector.tensor_tensor(out=out_rows[n][:, :, t, :], in0=out_acc[:], in1=b2_rows[:], op=ADD)
-            if n == N_CHUNKS - 1:
-                store(n, t, t + 1)
-            elif t == SUB_ROWS - 1:
-                store(n, 0, SUB_ROWS)
 
-        def store(n, t_from, t_to):
+        def store(n):
+            if not is_chunk(n):
+                return
             for o in range(COMPS):
-                rows = outs[o][n * CHUNK : (n + 1) * CHUNK, :].rearrange("(p t) f -> p t f", t=SUB_ROWS)
-                nc.sync.dma_start(out=rows[:, t_from:t_to, :], in_=out_rows[n][:, o, t_from:t_to, :])
+                rows = outs[o][n * CHUNK : (n + 1) * CHUNK, :]
+                nc.sync.dma_start(out=rows.rearrange("(p t) f -> p t f", t=SUB_ROWS), in_=out_rows[n][:, o, :, :])
 
         def run_round(n):
             regroup_h(n - 1)
             transpose_q(n + 1)
             quantise_q(n + 1, 0)
             layer_1_tile(n, 0)
-            layer_2_block(n - LAYER_2_LAG, 0)
+            layer_2_sub_row(n - LAYER_2_LAG, 0)
             quantise_h(n - 1)
             layer_1_tile(n, 1)
-            layer_2_block(n - LAYER_2_LAG, 1)
+            layer_2_sub_row(n - LAYER_2_LAG, 1)
             quantise_q(n + 1, 1)
             layer_1_tile(n, 2)
-            layer_2_block(n - LAYER_2_LAG, 2)
+            layer_2_sub_row(n - LAYER_2_LAG, 2)
             layer_1_tile(n, 3)
-            layer_2_block(n - LAYER_2_LAG, 3)
+            layer_2_sub_row(n - LAYER_2_LAG, 3)
+            store(n - LAYER_2_LAG)
 
         run_round(-1)
         sign_w2()

@@ -38,7 +38,7 @@ W1_PLANES = (
     ((1.0, K), (1.0, J), (-1.0, J), (-1.0, K)),
 )
 LAYER_2_LAG = 2
-SCALAR_COLUMNS = 192
+SCALAR_COLUMNS = 128
 COLUMN_RUN = 4
 
 FLOPS = 2 * ROWS * (COMPS * D_IN) * (COMPS * D_HID) + 2 * ROWS * (COMPS * D_HID) * (COMPS * D_OUT)
@@ -133,7 +133,7 @@ def tile_qmlp_t_kernel(
                 assert x < y
                 source = w1_t[b][:, x : y + 1 : y - x, :].rearrange("p u (i j) -> p j i u", j=PACK)
                 target = w1_words[:, g, :, o * QUADRANT : (o + 1) * QUADRANT, :]
-                if o % 2 == 0:
+                if b == 0:
                     nc.vector.tensor_copy(out=target, in_=source)
                 else:
                     nc.scalar.copy(out=target, in_=source)
@@ -176,27 +176,28 @@ def tile_qmlp_t_kernel(
 
         q_grouped, q_codes, q_scales = {}, {}, {}
         h_tiles, h_grouped, h_codes, h_scales = {}, {}, {}, {}
+        scalar_share = {}
         out_rows = {}
 
         def is_chunk(n):
             return 0 <= n < N_CHUNKS
 
-        def transpose_q(n):
+        def transpose_q(n, g):
             if not is_chunk(n):
                 return
-            q_grouped[n] = work.tile([P, L1_PASSES, CHUNK * PACK], BF16, name="q_grouped", align_bytes=64)
-            for g in range(L1_PASSES):
-                for half in range(SUB_ROWS // BANK_GROUPS):
-                    q_t = psum_s.tile([P, BANK_GROUPS, PAIRS, P], F32, tag="for_scalar")
-                    for a in range(BANK_GROUPS):
-                        for u in range(PAIRS):
-                            pairs = q_rows[n][:, PAIRS * g + u, BANK_GROUPS * half + a, :].bitcast(F32)
-                            nc.tensor.transpose(q_t[:, a, u, :], pairs, identity[:])
-                    width = BANK_GROUPS * P * PACK
-                    nc.scalar.copy(
-                        out=as_pairs(q_grouped[n][:, g, half * width : (half + 1) * width]),
-                        in_=q_t[:].rearrange("p a u r -> p a r u"),
-                    )
+            if g == 0:
+                q_grouped[n] = work.tile([P, L1_PASSES, CHUNK * PACK], BF16, name="q_grouped", align_bytes=64)
+            for half in range(SUB_ROWS // BANK_GROUPS):
+                q_t = psum_s.tile([P, BANK_GROUPS, PAIRS, P], F32, tag="for_scalar")
+                for a in range(BANK_GROUPS):
+                    for u in range(PAIRS):
+                        pairs = q_rows[n][:, PAIRS * g + u, BANK_GROUPS * half + a, :].bitcast(F32)
+                        nc.tensor.transpose(q_t[:, a, u, :], pairs, identity[:])
+                width = BANK_GROUPS * P * PACK
+                nc.scalar.copy(
+                    out=as_pairs(q_grouped[n][:, g, half * width : (half + 1) * width]),
+                    in_=q_t[:].rearrange("p a u r -> p a r u"),
+                )
 
         def quantise_q(n, g):
             if not is_chunk(n):
@@ -233,9 +234,14 @@ def tile_qmlp_t_kernel(
             target = h_grouped[n][:].rearrange("p (c i) j -> p c j i", i=COLUMN_RUN)
             source = h_tiles[n][:].rearrange("p j (c i) -> p c j i", i=COLUMN_RUN)
             split = SCALAR_COLUMNS // COLUMN_RUN if n >= LAYER_2_LAG else 0
-            if split > 0:
-                nc.scalar.copy(out=target[:, :split], in_=source[:, :split])
             nc.vector.tensor_copy(out=target[:, split:], in_=source[:, split:])
+            if split > 0:
+                scalar_share[n] = (target[:, :split], source[:, :split])
+
+        def regroup_scalar_share(n):
+            if n in scalar_share:
+                target, source = scalar_share[n]
+                nc.scalar.copy(out=target, in_=source)
 
         def quantise_h(n):
             if not is_chunk(n):
@@ -274,7 +280,9 @@ def tile_qmlp_t_kernel(
 
         def run_round(n):
             regroup_h(n - 1)
-            transpose_q(n + 1)
+            transpose_q(n + 1, 0)
+            regroup_scalar_share(n - 1)
+            transpose_q(n + 1, 1)
             quantise_q(n + 1, 0)
             layer_1_tile(n, 0)
             layer_2_sub_row(n - LAYER_2_LAG, 0)

@@ -93,9 +93,9 @@ def tile_qmlp_t_kernel(
         nc.scalar.activation(out=warm[:], in_=warm[:], func=RELU)
         load_chunk(0)
         load_chunk(1)
-        w2_in = const.tile([P, COMPS, D_HID], BF16)
-        for c in range(COMPS):
-            nc.sync.dma_start(out=w2_in[:, c, :], in_=w2[c])
+        w2_rows = const.tile([P, COMPS, COMPS, D_HID], BF16)
+        for o in range(COMPS):
+            nc.sync.dma_start(out=w2_rows[:, o, R, :], in_=w2[o])
         load_chunk(2)
         load_chunk(3)
         b2_rows = const.tile([P, COMPS, D_OUT], BF16)
@@ -144,25 +144,26 @@ def tile_qmlp_t_kernel(
                 in_=w1_words[:, g, :, :, :].rearrange("p j m u -> p (j m u)").bitcast(BF16),
             )
 
-        w2_rows = const.tile([P, COMPS, COMPS * D_HID], BF16)
         w2_grouped = const.tile([P, COMPS * D_OUT * PACK], BF16, align_bytes=64)
         w2_codes = const.tile([P, COMPS * D_OUT], U32, align_bytes=64)
         w2_scales = const.tile([P, COMPS * D_OUT], U8, align_bytes=64)
 
         def sign_w2():
-            for o in range(COMPS):
-                for c in range(COMPS):
-                    nc.vector.tensor_scalar_mul(
-                        out=w2_rows[:, o, c * D_HID : (c + 1) * D_HID],
-                        in0=w2_in[:, o ^ c, :],
-                        scalar1=HAMILTON_SIGN[o][c],
-                    )
+            nc.vector.tensor_scalar_mul(out=w2_rows[:, R, I:, :], in0=w2_rows[:, I:, R, :], scalar1=-1.0)
+            diagonal = w2_rows[:].rearrange("f o c k -> f (o c) k")[:, COMPS + 1 :: COMPS + 1, :]
+            nc.vector.tensor_copy(out=diagonal, in_=w2_rows[:, R : R + 1, R, :].to_broadcast([P, COMPS - 1, D_HID]))
+            for o in (I, J, K):
+                for c in (I, J, K):
+                    if o != c:
+                        nc.vector.tensor_scalar_mul(
+                            out=w2_rows[:, o, c, :], in0=w2_rows[:, o ^ c, R, :], scalar1=HAMILTON_SIGN[o][c]
+                        )
 
         def transpose_w2():
             for half in range(COMPS // BANK_GROUPS):
                 w2_t = psum_v.tile([P, BANK_GROUPS, PAIRS, D_OUT], F32, tag="for_vector")
                 for a in range(BANK_GROUPS):
-                    pairs = w2_rows[:, BANK_GROUPS * half + a, :].bitcast(F32).rearrange("f (p u) -> f u p", u=PAIRS)
+                    pairs = w2_rows[:, BANK_GROUPS * half + a, :, :].rearrange("f c k -> f (c k)").bitcast(F32).rearrange("f (p u) -> f u p", u=PAIRS)
                     for u in range(PAIRS):
                         nc.tensor.transpose(w2_t[:, a, u, :], pairs[:, u, :], identity[:])
                 width = BANK_GROUPS * D_OUT * PACK
@@ -188,13 +189,16 @@ def tile_qmlp_t_kernel(
             if g == 0:
                 q_grouped[n] = work.tile([P, L1_PASSES, CHUNK * PACK], BF16, name="q_grouped", align_bytes=64)
             for half in range(SUB_ROWS // BANK_GROUPS):
-                q_t = psum_s.tile([P, BANK_GROUPS, PAIRS, P], F32, tag="for_scalar")
+                on_vector = half == 1 and n <= LAYER_2_LAG
+                pool, tag = (psum_v, "for_vector") if on_vector else (psum_s, "for_scalar")
+                q_t = pool.tile([P, BANK_GROUPS, PAIRS, P], F32, name="q_t", tag=tag)
                 for a in range(BANK_GROUPS):
                     for u in range(PAIRS):
                         pairs = q_rows[n][:, PAIRS * g + u, BANK_GROUPS * half + a, :].bitcast(F32)
                         nc.tensor.transpose(q_t[:, a, u, :], pairs, identity[:])
                 width = BANK_GROUPS * P * PACK
-                nc.scalar.copy(
+                copy = nc.vector.tensor_copy if on_vector else nc.scalar.copy
+                copy(
                     out=as_pairs(q_grouped[n][:, g, half * width : (half + 1) * width]),
                     in_=q_t[:].rearrange("p a u r -> p a r u"),
                 )
@@ -233,7 +237,8 @@ def tile_qmlp_t_kernel(
             h_grouped[n] = work.tile([P, CHUNK, PACK], BF16, name="h_grouped", align_bytes=64)
             target = h_grouped[n][:].rearrange("p (c i) j -> p c j i", i=COLUMN_RUN)
             source = h_tiles[n][:].rearrange("p j (c i) -> p c j i", i=COLUMN_RUN)
-            split = SCALAR_COLUMNS // COLUMN_RUN if n >= LAYER_2_LAG else 0
+            columns = CHUNK // 2 if n == N_CHUNKS - 1 else SCALAR_COLUMNS if n >= LAYER_2_LAG else 0
+            split = columns // COLUMN_RUN
             nc.vector.tensor_copy(out=target[:, split:], in_=source[:, split:])
             if split > 0:
                 scalar_share[n] = (target[:, :split], source[:, :split])

@@ -276,12 +276,12 @@ def tile_qmlp_t_kernel(
             )
             nc.vector.tensor_tensor(out=out_rows[n][:, :, t, :], in0=out_acc[:], in1=b2_rows[:], op=ADD)
 
-        def store(n):
+        def store(n, first, last):
             if not is_chunk(n):
                 return
             for o in range(COMPS):
-                rows = outs[o][n * CHUNK : (n + 1) * CHUNK, :]
-                nc.sync.dma_start(out=rows.rearrange("(p t) f -> p t f", t=SUB_ROWS), in_=out_rows[n][:, o, :, :])
+                rows = outs[o][n * CHUNK : (n + 1) * CHUNK, :].rearrange("(p t) f -> p t f", t=SUB_ROWS)
+                nc.sync.dma_start(out=rows[:, first : last + 1, :], in_=out_rows[n][:, o, first : last + 1, :])
 
         def run_round(n):
             regroup_h(n - 1)
@@ -294,12 +294,15 @@ def tile_qmlp_t_kernel(
             quantise_h(n - 1)
             layer_1_tile(n, 1)
             layer_2_sub_row(n - LAYER_2_LAG, 1)
+            split = n - LAYER_2_LAG >= N_CHUNKS - 2
+            if split:
+                store(n - LAYER_2_LAG, 0, 1)
             quantise_q(n + 1, 1)
             layer_1_tile(n, 2)
             layer_2_sub_row(n - LAYER_2_LAG, 2)
             layer_1_tile(n, 3)
             layer_2_sub_row(n - LAYER_2_LAG, 3)
-            store(n - LAYER_2_LAG)
+            store(n - LAYER_2_LAG, 2 if split else 0, 3)
 
         run_round(-1)
         sign_w2()

@@ -111,6 +111,16 @@ def tile_qmlp_t_kernel(
                 in_=b1[o].rearrange("(i j) -> i j", j=PACK),
             )
 
+        zeros = const.tile([P, CHUNK], BF16)
+        nc.vector.memset(zeros[:], 0.0)
+
+        def keep_clock(matmuls):
+            idle_acc = psum_v.tile([P, CHUNK], F32, name="idle_acc", tag="for_vector")
+            for m in range(matmuls):
+                nc.tensor.matmul(out=idle_acc[:], lhsT=zeros[:, :P], rhs=zeros[:], start=True, stop=True)
+
+        keep_clock(4)
+
         w1_minus = const.tile([P, COMPS, D_IN], BF16)
         nc.vector.tensor_scalar_mul(out=w1_minus[:, I:, :], in0=w1_plus[:, I:, :], scalar1=-1.0)
         w1_signed = {1.0: w1_plus, -1.0: w1_minus}
@@ -120,6 +130,7 @@ def tile_qmlp_t_kernel(
                 for x, (sign, c) in enumerate(planes):
                     if sign == wanted:
                         nc.tensor.transpose(w1_t[b][:, x, :], w1_signed[sign][:, c, :].bitcast(F32), identity[:])
+        keep_clock(2)
         w1_words = const.tile([P, L1_PASSES, PACK, P, PAIRS], F32, align_bytes=64)
         w1_codes = const.tile([P, L1_PASSES, PACK, P], U32, align_bytes=64)
         w1_scales = const.tile([P, L1_PASSES, PACK, P], U8, align_bytes=64)
@@ -286,8 +297,12 @@ def tile_qmlp_t_kernel(
         def run_round(n):
             regroup_h(n - 1)
             transpose_q(n + 1, 0)
+            if n < 0:
+                keep_clock(2)
             regroup_scalar_share(n - 1)
             transpose_q(n + 1, 1)
+            if n < 0:
+                keep_clock(2)
             quantise_q(n + 1, 0)
             layer_1_tile(n, 0)
             layer_2_sub_row(n - LAYER_2_LAG, 0)

@@ -119,7 +119,7 @@ def tile_qmlp_t_kernel(
             for m in range(matmuls):
                 nc.tensor.matmul(out=idle_acc[:], lhsT=zeros[:, :P], rhs=zeros[:], start=True, stop=True)
 
-        keep_clock(4)
+        keep_clock(5)
 
         w1_minus = const.tile([P, COMPS, D_IN], BF16)
         nc.vector.tensor_scalar_mul(out=w1_minus[:, I:, :], in0=w1_plus[:, I:, :], scalar1=-1.0)
@@ -200,7 +200,7 @@ def tile_qmlp_t_kernel(
             if g == 0:
                 q_grouped[n] = work.tile([P, L1_PASSES, CHUNK * PACK], BF16, name="q_grouped", align_bytes=64)
             for half in range(SUB_ROWS // BANK_GROUPS):
-                on_vector = half == 1 and n <= LAYER_2_LAG
+                on_vector = half == 1 and g == L1_PASSES - 1 and n <= LAYER_2_LAG
                 pool, tag = (psum_v, "for_vector") if on_vector else (psum_s, "for_scalar")
                 q_t = pool.tile([P, BANK_GROUPS, PAIRS, P], F32, name="q_t", tag=tag)
                 for a in range(BANK_GROUPS):
@@ -309,7 +309,7 @@ def tile_qmlp_t_kernel(
             quantise_h(n - 1)
             layer_1_tile(n, 1)
             layer_2_sub_row(n - LAYER_2_LAG, 1)
-            split = n - LAYER_2_LAG >= N_CHUNKS - 2
+            split = n - LAYER_2_LAG >= N_CHUNKS // 2
             if split:
                 store(n - LAYER_2_LAG, 0, 1)
             quantise_q(n + 1, 1)

@@ -39,7 +39,7 @@ W1_PLANES = (
 )
 LAYER_2_LAG = 2
 SCALAR_COLUMNS = 128
-COLUMN_RUN = 4
+COLUMN_RUN = 8
 
 FLOPS = 2 * ROWS * (COMPS * D_IN) * (COMPS * D_HID) + 2 * ROWS * (COMPS * D_HID) * (COMPS * D_OUT)
 

@@ -131,9 +131,9 @@ def tile_qmlp_t_kernel(
                     if sign == wanted:
                         nc.tensor.transpose(w1_t[b][:, x, :], w1_signed[sign][:, c, :].bitcast(F32), identity[:])
         keep_clock(2)
-        w1_words = const.tile([P, L1_PASSES, PACK, P, PAIRS], F32, align_bytes=64)
-        w1_codes = const.tile([P, L1_PASSES, PACK, P], U32, align_bytes=64)
-        w1_scales = const.tile([P, L1_PASSES, PACK, P], U8, align_bytes=64)
+        w1_words = const.tile([P, L1_PASSES, PACK, P, PAIRS], F32, align_bytes=256)
+        w1_codes = const.tile([P, L1_PASSES, PACK, P], U32, align_bytes=256)
+        w1_scales = const.tile([P, L1_PASSES, PACK, P], U8, align_bytes=256)
         for g in range(L1_PASSES):
             for o in range(COMPS):
                 first = (HAMILTON_SIGN[o][PAIRS * g], o ^ (PAIRS * g))
@@ -155,9 +155,9 @@ def tile_qmlp_t_kernel(
                 in_=w1_words[:, g, :, :, :].rearrange("p j m u -> p (j m u)").bitcast(BF16),
             )
 
-        w2_grouped = const.tile([P, COMPS * D_OUT * PACK], BF16, align_bytes=64)
-        w2_codes = const.tile([P, COMPS * D_OUT], U32, align_bytes=64)
-        w2_scales = const.tile([P, COMPS * D_OUT], U8, align_bytes=64)
+        w2_grouped = const.tile([P, COMPS * D_OUT * PACK], BF16, align_bytes=256)
+        w2_codes = const.tile([P, COMPS * D_OUT], U32, align_bytes=256)
+        w2_scales = const.tile([P, COMPS * D_OUT], U8, align_bytes=256)
 
         def sign_w2():
             nc.vector.tensor_scalar_mul(out=w2_rows[:, R, I:, :], in0=w2_rows[:, I:, R, :], scalar1=-1.0)
@@ -198,7 +198,7 @@ def tile_qmlp_t_kernel(
             if not is_chunk(n):
                 return
             if g == 0:
-                q_grouped[n] = work.tile([P, L1_PASSES, CHUNK * PACK], BF16, name="q_grouped", align_bytes=64)
+                q_grouped[n] = work.tile([P, L1_PASSES, CHUNK * PACK], BF16, name="q_grouped", align_bytes=256)
             for half in range(SUB_ROWS // BANK_GROUPS):
                 on_vector = half == 1 and g == L1_PASSES - 1 and n <= LAYER_2_LAG
                 pool, tag = (psum_v, "for_vector") if on_vector else (psum_s, "for_scalar")
@@ -218,8 +218,8 @@ def tile_qmlp_t_kernel(
             if not is_chunk(n):
                 return
             if g == 0:
-                q_codes[n] = work.tile([P, L1_PASSES, CHUNK], U32, name="q_codes", align_bytes=64)
-                q_scales[n] = work.tile([P, L1_PASSES, CHUNK], U8, name="q_scales", align_bytes=64)
+                q_codes[n] = work.tile([P, L1_PASSES, CHUNK], U32, name="q_codes", align_bytes=256)
+                q_scales[n] = work.tile([P, L1_PASSES, CHUNK], U8, name="q_scales", align_bytes=256)
             nc.vector.quantize_mx(
                 out=q_codes[n][:, g, :].bitcast(FP8X4), scales=q_scales[n][:, g, :], in_=q_grouped[n][:, g, :]
             )
@@ -245,7 +245,7 @@ def tile_qmlp_t_kernel(
         def regroup_h(n):
             if not is_chunk(n):
                 return
-            h_grouped[n] = work.tile([P, CHUNK, PACK], BF16, name="h_grouped", align_bytes=64)
+            h_grouped[n] = work.tile([P, CHUNK, PACK], BF16, name="h_grouped", align_bytes=256)
             target = h_grouped[n][:].rearrange("p (c i) j -> p c j i", i=COLUMN_RUN)
             source = h_tiles[n][:].rearrange("p j (c i) -> p c j i", i=COLUMN_RUN)
             columns = CHUNK // 2 if n == N_CHUNKS - 1 else SCALAR_COLUMNS if n >= LAYER_2_LAG else 0
@@ -262,8 +262,8 @@ def tile_qmlp_t_kernel(
         def quantise_h(n):
             if not is_chunk(n):
                 return
-            h_codes[n] = work.tile([P, CHUNK], U32, name="h_codes", align_bytes=64)
-            h_scales[n] = work.tile([P, CHUNK], U8, name="h_scales", align_bytes=64)
+            h_codes[n] = work.tile([P, CHUNK], U32, name="h_codes", align_bytes=256)
+            h_scales[n] = work.tile([P, CHUNK], U8, name="h_scales", align_bytes=256)
             nc.vector.quantize_mx(
                 out=h_codes[n][:].bitcast(FP8X4),
                 scales=h_scales[n][:],

@@ -38,7 +38,7 @@ W1_PLANES = (
     ((1.0, K), (1.0, J), (-1.0, J), (-1.0, K)),
 )
 LAYER_2_LAG = 2
-SCALAR_COLUMNS = 128
+SCALAR_COLUMNS = 160
 COLUMN_RUN = 8
 
 FLOPS = 2 * ROWS * (COMPS * D_IN) * (COMPS * D_HID) + 2 * ROWS * (COMPS * D_HID) * (COMPS * D_OUT)
@@ -69,7 +69,8 @@ def tile_qmlp_t_kernel(
         const = stack.enter_context(tc.tile_pool(name="const", bufs=1))
         q_pool = stack.enter_context(tc.tile_pool(name="q_rows", bufs=N_CHUNKS))
         work = stack.enter_context(tc.tile_pool(name="work", bufs=2))
-        out_pool = stack.enter_context(tc.tile_pool(name="out_rows", bufs=3))
+        codes_pool = stack.enter_context(tc.tile_pool(name="codes", bufs=N_CHUNKS))
+        out_pool = stack.enter_context(tc.tile_pool(name="out_rows", bufs=5))
         psum_s = stack.enter_context(tc.psum_pool(name="psum_s", bufs=5))
         psum_v = stack.enter_context(tc.psum_pool(name="psum_v", bufs=3))
         stack.enter_context(tc.manual_schedule())
@@ -218,8 +219,8 @@ def tile_qmlp_t_kernel(
             if not is_chunk(n):
                 return
             if g == 0:
-                q_codes[n] = work.tile([P, L1_PASSES, CHUNK], U32, name="q_codes", align_bytes=256)
-                q_scales[n] = work.tile([P, L1_PASSES, CHUNK], U8, name="q_scales", align_bytes=256)
+                q_codes[n] = codes_pool.tile([P, L1_PASSES, CHUNK], U32, name="q_codes", align_bytes=256)
+                q_scales[n] = codes_pool.tile([P, L1_PASSES, CHUNK], U8, name="q_scales", align_bytes=256)
             nc.vector.quantize_mx(
                 out=q_codes[n][:, g, :].bitcast(FP8X4), scales=q_scales[n][:, g, :], in_=q_grouped[n][:, g, :]
             )
@@ -262,8 +263,8 @@ def tile_qmlp_t_kernel(
         def quantise_h(n):
             if not is_chunk(n):
                 return
-            h_codes[n] = work.tile([P, CHUNK], U32, name="h_codes", align_bytes=256)
-            h_scales[n] = work.tile([P, CHUNK], U8, name="h_scales", align_bytes=256)
+            h_codes[n] = codes_pool.tile([P, CHUNK], U32, name="h_codes", align_bytes=256)
+            h_scales[n] = codes_pool.tile([P, CHUNK], U8, name="h_scales", align_bytes=256)
             nc.vector.quantize_mx(
                 out=h_codes[n][:].bitcast(FP8X4),
                 scales=h_scales[n][:],

from contextlib import ExitStack

import concourse.mybir as mybir
from concourse.masks import make_identity

F32 = mybir.dt.float32
BF16 = mybir.dt.bfloat16
U32 = mybir.dt.uint32
U8 = mybir.dt.uint8
FP8X4 = mybir.dt.float8_e4m3fn_x4
RELU = mybir.ActivationFunctionType.Relu
ADD = mybir.AluOpType.add

P = 128
PACK = 4
PAIRS = 2
COMPS = 4
ROWS = 4096
D_IN = 256
D_HID = 128
D_OUT = 128
L1_PASSES = COMPS * D_IN // (P * PACK)
SUB_ROWS = 4
CHUNK = P * SUB_ROWS
N_CHUNKS = ROWS // CHUNK
QUADRANT = P // COMPS
BANK_GROUPS = 2

R, I, J, K = range(COMPS)
HAMILTON_SIGN = (
    (1.0, -1.0, -1.0, -1.0),
    (1.0, 1.0, 1.0, -1.0),
    (1.0, -1.0, 1.0, 1.0),
    (1.0, 1.0, -1.0, 1.0),
)
W1_PLANES = (
    ((1.0, R), (1.0, I), (-1.0, I), (1.0, R)),
    ((1.0, K), (1.0, J), (-1.0, J), (-1.0, K)),
)
LAYER_2_LAG = 2
SCALAR_COLUMNS = 160
COLUMN_RUN = 8

FLOPS = 2 * ROWS * (COMPS * D_IN) * (COMPS * D_HID) + 2 * ROWS * (COMPS * D_HID) * (COMPS * D_OUT)


def as_pairs(values):
    return values.bitcast(F32).rearrange("p (a r u) -> p a r u", a=BANK_GROUPS, u=PAIRS)


def tile_qmlp_t_kernel(
    tc,
    q_r, q_i, q_j, q_k,
    W1_r, W1_i, W1_j, W1_k,
    b1_r, b1_i, b1_j, b1_k,
    W2_r, W2_i, W2_j, W2_k,
    b2_r, b2_i, b2_j, b2_k,
    out_0, out_1, out_2, out_3,
):
    nc = tc.nc
    q = (q_r, q_i, q_j, q_k)
    w1 = (W1_r, W1_i, W1_j, W1_k)
    b1 = (b1_r, b1_i, b1_j, b1_k)
    w2 = (W2_r, W2_i, W2_j, W2_k)
    b2 = (b2_r, b2_i, b2_j, b2_k)
    outs = (out_0, out_1, out_2, out_3)

    with ExitStack() as stack:
        const = stack.enter_context(tc.tile_pool(name="const", bufs=1))
        q_pool = stack.enter_context(tc.tile_pool(name="q_rows", bufs=N_CHUNKS))
        work = stack.enter_context(tc.tile_pool(name="work", bufs=2))
        codes_pool = stack.enter_context(tc.tile_pool(name="codes", bufs=N_CHUNKS))
        out_pool = stack.enter_context(tc.tile_pool(name="out_rows", bufs=5))
        psum_s = stack.enter_context(tc.psum_pool(name="psum_s", bufs=5))
        psum_v = stack.enter_context(tc.psum_pool(name="psum_v", bufs=3))
        stack.enter_context(tc.manual_schedule())

        identity = const.tile([P, P], F32)
        make_identity(nc, identity[:])

        q_rows = {}

        def load_chunk(n):
            q_rows[n] = q_pool.tile([P, COMPS, SUB_ROWS, D_IN], BF16, name="q_rows")
            for c in range(COMPS):
                rows = q[c][n * CHUNK : (n + 1) * CHUNK, :]
                nc.sync.dma_start(out=q_rows[n][:, c, :, :], in_=rows.rearrange("(p t) k -> p t k", t=SUB_ROWS))

        w1_plus = const.tile([P, COMPS, D_IN], BF16)
        for c in range(COMPS):
            nc.sync.dma_start(out=w1_plus[:, c, :], in_=w1[c])
        warm = const.tile([P, 1], F32)
        nc.vector.memset(warm[:], 0.0)
        nc.scalar.activation(out=warm[:], in_=warm[:], func=RELU)
        load_chunk(0)
        load_chunk(1)
        w2_rows = const.tile([P, COMPS, COMPS, D_HID], BF16)
        for o in range(COMPS):
            nc.sync.dma_start(out=w2_rows[:, o, R, :], in_=w2[o])
        load_chunk(2)
        load_chunk(3)
        b2_rows = const.tile([P, COMPS, D_OUT], BF16)
        for o in range(COMPS):
            nc.sync.dma_start(out=b2_rows[:, o, :], in_=b2[o].partition_broadcast(P))
        for n in range(4, N_CHUNKS):
            load_chunk(n)

        b1_cols = const.tile([P, PACK], BF16)
        for o in range(COMPS):
            nc.gpsimd.dma_start(
                out=b1_cols[o * QUADRANT : (o + 1) * QUADRANT, :],
                in_=b1[o].rearrange("(i j) -> i j", j=PACK),
            )

        zeros = const.tile([P, CHUNK], BF16)
        nc.vector.memset(zeros[:], 0.0)

        def keep_clock(matmuls):
            idle_acc = psum_v.tile([P, CHUNK], F32, name="idle_acc", tag="for_vector")
            for m in range(matmuls):
                nc.tensor.matmul(out=idle_acc[:], lhsT=zeros[:, :P], rhs=zeros[:], start=True, stop=True)

        keep_clock(5)

        w1_minus = const.tile([P, COMPS, D_IN], BF16)
        nc.vector.tensor_scalar_mul(out=w1_minus[:, I:, :], in0=w1_plus[:, I:, :], scalar1=-1.0)
        w1_signed = {1.0: w1_plus, -1.0: w1_minus}
        w1_t = [psum_s.tile([P, COMPS, D_HID], F32, name="w1_t", tag="for_scalar") for planes in W1_PLANES]
        for wanted in (1.0, -1.0):
            for b, planes in enumerate(W1_PLANES):
                for x, (sign, c) in enumerate(planes):
                    if sign == wanted:
                        nc.tensor.transpose(w1_t[b][:, x, :], w1_signed[sign][:, c, :].bitcast(F32), identity[:])
        keep_clock(2)
        w1_words = const.tile([P, L1_PASSES, PACK, P, PAIRS], F32, align_bytes=256)
        w1_codes = const.tile([P, L1_PASSES, PACK, P], U32, align_bytes=256)
        w1_scales = const.tile([P, L1_PASSES, PACK, P], U8, align_bytes=256)
        for g in range(L1_PASSES):
            for o in range(COMPS):
                first = (HAMILTON_SIGN[o][PAIRS * g], o ^ (PAIRS * g))
                second = (HAMILTON_SIGN[o][PAIRS * g + 1], o ^ (PAIRS * g + 1))
                b = first[1] // PAIRS
                x = W1_PLANES[b].index(first)
                y = COMPS - 1 - W1_PLANES[b][::-1].index(second)
                assert x < y
                source = w1_t[b][:, x : y + 1 : y - x, :].rearrange("p u (i j) -> p j i u", j=PACK)
                target = w1_words[:, g, :, o * QUADRANT : (o + 1) * QUADRANT, :]
                if b == 0:
                    nc.vector.tensor_copy(out=target, in_=source)
                else:
                    nc.scalar.copy(out=target, in_=source)
        for g in range(L1_PASSES):
            nc.vector.quantize_mx(
                out=w1_codes[:, g, :, :].rearrange("p j m -> p (j m)").bitcast(FP8X4),
                scales=w1_scales[:, g, :, :].rearrange("p j m -> p (j m)"),
                in_=w1_words[:, g, :, :, :].rearrange("p j m u -> p (j m u)").bitcast(BF16),
            )

        w2_grouped = const.tile([P, COMPS * D_OUT * PACK], BF16, align_bytes=256)
        w2_codes = const.tile([P, COMPS * D_OUT], U32, align_bytes=256)
        w2_scales = const.tile([P, COMPS * D_OUT], U8, align_bytes=256)

        def sign_w2():
            nc.vector.tensor_scalar_mul(out=w2_rows[:, R, I:, :], in0=w2_rows[:, I:, R, :], scalar1=-1.0)
            diagonal = w2_rows[:].rearrange("f o c k -> f (o c) k")[:, COMPS + 1 :: COMPS + 1, :]
            nc.vector.tensor_copy(out=diagonal, in_=w2_rows[:, R : R + 1, R, :].to_broadcast([P, COMPS - 1, D_HID]))
            for o in (I, J, K):
                for c in (I, J, K):
                    if o != c:
                        nc.vector.tensor_scalar_mul(
                            out=w2_rows[:, o, c, :], in0=w2_rows[:, o ^ c, R, :], scalar1=HAMILTON_SIGN[o][c]
                        )

        def transpose_w2():
            for half in range(COMPS // BANK_GROUPS):
                w2_t = psum_v.tile([P, BANK_GROUPS, PAIRS, D_OUT], F32, tag="for_vector")
                for a in range(BANK_GROUPS):
                    pairs = w2_rows[:, BANK_GROUPS * half + a, :, :].rearrange("f c k -> f (c k)").bitcast(F32).rearrange("f (p u) -> f u p", u=PAIRS)
                    for u in range(PAIRS):
                        nc.tensor.transpose(w2_t[:, a, u, :], pairs[:, u, :], identity[:])
                width = BANK_GROUPS * D_OUT * PACK
                nc.scalar.copy(
                    out=as_pairs(w2_grouped[:, half * width : (half + 1) * width]),
                    in_=w2_t[:].rearrange("p a u r -> p a r u"),
                )

        def quantise_w2():
            nc.vector.quantize_mx(out=w2_codes[:].bitcast(FP8X4), scales=w2_scales[:], in_=w2_grouped[:])

        q_grouped, q_codes, q_scales = {}, {}, {}
        h_tiles, h_grouped, h_codes, h_scales = {}, {}, {}, {}
        scalar_share = {}
        out_rows = {}

        def is_chunk(n):
            return 0 <= n < N_CHUNKS

        def transpose_q(n, g):
            if not is_chunk(n):
                return
            if g == 0:
                q_grouped[n] = work.tile([P, L1_PASSES, CHUNK * PACK], BF16, name="q_grouped", align_bytes=256)
            for half in range(SUB_ROWS // BANK_GROUPS):
                on_vector = half == 1 and g == L1_PASSES - 1 and n <= LAYER_2_LAG
                pool, tag = (psum_v, "for_vector") if on_vector else (psum_s, "for_scalar")
                q_t = pool.tile([P, BANK_GROUPS, PAIRS, P], F32, name="q_t", tag=tag)
                for a in range(BANK_GROUPS):
                    for u in range(PAIRS):
                        pairs = q_rows[n][:, PAIRS * g + u, BANK_GROUPS * half + a, :].bitcast(F32)
                        nc.tensor.transpose(q_t[:, a, u, :], pairs, identity[:])
                width = BANK_GROUPS * P * PACK
                copy = nc.vector.tensor_copy if on_vector else nc.scalar.copy
                copy(
                    out=as_pairs(q_grouped[n][:, g, half * width : (half + 1) * width]),
                    in_=q_t[:].rearrange("p a u r -> p a r u"),
                )

        def quantise_q(n, g):
            if not is_chunk(n):
                return
            if g == 0:
                q_codes[n] = codes_pool.tile([P, L1_PASSES, CHUNK], U32, name="q_codes", align_bytes=256)
                q_scales[n] = codes_pool.tile([P, L1_PASSES, CHUNK], U8, name="q_scales", align_bytes=256)
            nc.vector.quantize_mx(
                out=q_codes[n][:, g, :].bitcast(FP8X4), scales=q_scales[n][:, g, :], in_=q_grouped[n][:, g, :]
            )

        def layer_1_tile(n, j):
            if not is_chunk(n):
                return
            if j == 0:
                h_tiles[n] = work.tile([P, PACK, CHUNK], BF16, name="h_tiles")
            h_acc = psum_s.tile([P, CHUNK], F32, tag="for_scalar")
            for g in range(L1_PASSES):
                nc.tensor.matmul_mx(
                    out=h_acc[:],
                    lhsT=w1_codes[:, g, j, :].bitcast(FP8X4),
                    lhsT_scale=w1_scales[:, g, j, :],
                    rhs=q_codes[n][:, g, :].bitcast(FP8X4),
                    rhs_scale=q_scales[n][:, g, :],
                    start=(g == 0),
                    stop=(g == L1_PASSES - 1),
                )
            nc.scalar.activation(out=h_tiles[n][:, j, :], in_=h_acc[:], func=RELU, bias=b1_cols[:, j : j + 1])

        def regroup_h(n):
            if not is_chunk(n):
                return
            h_grouped[n] = work.tile([P, CHUNK, PACK], BF16, name="h_grouped", align_bytes=256)
            target = h_grouped[n][:].rearrange("p (c i) j -> p c j i", i=COLUMN_RUN)
            source = h_tiles[n][:].rearrange("p j (c i) -> p c j i", i=COLUMN_RUN)
            columns = CHUNK // 2 if n == N_CHUNKS - 1 else SCALAR_COLUMNS if n >= LAYER_2_LAG else 0
            split = columns // COLUMN_RUN
            nc.vector.tensor_copy(out=target[:, split:], in_=source[:, split:])
            if split > 0:
                scalar_share[n] = (target[:, :split], source[:, :split])

        def regroup_scalar_share(n):
            if n in scalar_share:
                target, source = scalar_share[n]
                nc.scalar.copy(out=target, in_=source)

        def quantise_h(n):
            if not is_chunk(n):
                return
            h_codes[n] = codes_pool.tile([P, CHUNK], U32, name="h_codes", align_bytes=256)
            h_scales[n] = codes_pool.tile([P, CHUNK], U8, name="h_scales", align_bytes=256)
            nc.vector.quantize_mx(
                out=h_codes[n][:].bitcast(FP8X4),
                scales=h_scales[n][:],
                in_=h_grouped[n][:].rearrange("p n j -> p (n j)"),
            )

        def layer_2_sub_row(n, t):
            if not is_chunk(n):
                return
            if t == 0:
                out_rows[n] = out_pool.tile([P, COMPS, SUB_ROWS, D_OUT], F32, name="out_rows")
            out_acc = psum_v.tile([P, COMPS, D_OUT], F32, tag="for_vector")
            nc.tensor.matmul_mx(
                out=out_acc[:].rearrange("p o f -> p (o f)"),
                lhsT=h_codes[n][:, t * P : (t + 1) * P].bitcast(FP8X4),
                lhsT_scale=h_scales[n][:, t * P : (t + 1) * P],
                rhs=w2_codes[:].bitcast(FP8X4),
                rhs_scale=w2_scales[:],
                start=True,
                stop=True,
            )
            nc.vector.tensor_tensor(out=out_rows[n][:, :, t, :], in0=out_acc[:], in1=b2_rows[:], op=ADD)

        def store(n, first, last):
            if not is_chunk(n):
                return
            for o in range(COMPS):
                rows = outs[o][n * CHUNK : (n + 1) * CHUNK, :].rearrange("(p t) f -> p t f", t=SUB_ROWS)
                nc.sync.dma_start(out=rows[:, first : last + 1, :], in_=out_rows[n][:, o, first : last + 1, :])

        def run_round(n):
            regroup_h(n - 1)
            transpose_q(n + 1, 0)
            if n < 0:
                keep_clock(2)
            regroup_scalar_share(n - 1)
            transpose_q(n + 1, 1)
            if n < 0:
                keep_clock(2)
            quantise_q(n + 1, 0)
            layer_1_tile(n, 0)
            layer_2_sub_row(n - LAYER_2_LAG, 0)
            quantise_h(n - 1)
            layer_1_tile(n, 1)
            layer_2_sub_row(n - LAYER_2_LAG, 1)
            split = n - LAYER_2_LAG >= N_CHUNKS // 2
            if split:
                store(n - LAYER_2_LAG, 0, 1)
            quantise_q(n + 1, 1)
            layer_1_tile(n, 2)
            layer_2_sub_row(n - LAYER_2_LAG, 2)
            layer_1_tile(n, 3)
            layer_2_sub_row(n - LAYER_2_LAG, 3)
            store(n - LAYER_2_LAG, 2 if split else 0, 3)

        run_round(-1)
        sign_w2()
        run_round(0)
        transpose_w2()
        run_round(1)
        quantise_w2()
        for n in range(LAYER_2_LAG, N_CHUNKS + LAYER_2_LAG):
            run_round(n)
